import numpy as np
import ml_dtypes


def mxq(x, axis, fmt="e4m3"):
    dtype, down = {"e4m3": (ml_dtypes.float8_e4m3fn, 7), "e5m2": (ml_dtypes.float8_e5m2, 14)}[fmt]
    v = np.moveaxis(np.asarray(x, np.float32).astype(ml_dtypes.bfloat16).astype(np.float64), axis, -1)
    blocks = v.reshape(v.shape[:-1] + (-1, 32))
    amax = np.abs(blocks).max(-1, keepdims=True)
    byte = np.maximum(np.where(amax > 0, np.frexp(amax)[1] - 1 + 127, 0) - down, 1)
    scale = np.exp2(byte - 127.0)
    codes = (blocks / scale).astype(np.float32).astype(dtype).astype(np.float64)
    return np.moveaxis((codes * scale).reshape(v.shape), -1, axis)


WIDE = False


def mx_kscale(k):
    if not WIDE:
        return np.ones(k)
    levels = np.array([10, -10, 5, -5, 0])
    a = np.random.permutation(np.resize(levels, k // 512 * 4)).reshape(k // 512, 4)
    idx = np.arange(k)
    return np.exp2(a[idx // 512, idx % 128 // 32])


BF16 = ml_dtypes.bfloat16


def bf(x):
    return np.asarray(x, np.float32).astype(BF16)


def f64(x):
    return np.asarray(x).astype(np.float64)


E2M1 = np.array([0.0, 0.5, 1.0, 1.5, 2.0, 3.0, 4.0, 6.0, -0.0, -0.5, -1.0, -1.5, -2.0, -3.0, -4.0, -6.0])


def pack_weight(w, fmt):
    k, n = w.shape
    w = f64(bf(w)).reshape(k // 32, 32, n)
    amax = np.abs(w).max(1)
    if fmt == "e4m3":
        byte = np.frexp(amax)[1] - 1 + 127 - 7
    else:
        mant, ex = np.frexp(amax / 6.0)
        byte = np.where(mant > 0.5, ex, ex - 1) + 127
    byte = np.clip(np.where(amax > 0, byte, 1), 1, 254)
    scaled = (w * np.exp2(127.0 - byte)[:, None, :]).reshape(k, n).astype(np.float32)
    by_word = np.ascontiguousarray(scaled.reshape(k // 512, 128, 4, n).transpose(0, 1, 3, 2))
    if fmt == "e4m3":
        words = by_word.astype(ml_dtypes.float8_e4m3fn).view(np.uint8)
    else:
        c = by_word.astype(ml_dtypes.float4_e2m1fn).view(np.uint8) & 0xF
        words = c[..., 0::2] | (c[..., 1::2] << 4)
    return np.ascontiguousarray(words), np.ascontiguousarray(byte.astype(np.uint8).reshape(k // 512, 16, n))


def unpack_weight(words, scales, fmt):
    g, p, n, _ = words.shape
    if fmt == "e4m3":
        vals = np.ascontiguousarray(words).view(ml_dtypes.float8_e4m3fn).astype(np.float64)
    else:
        nib = np.empty((g, p, n, 4), np.uint8)
        nib[..., 0::2] = words & 0xF
        nib[..., 1::2] = words >> 4
        vals = E2M1[nib]
    vals = vals * np.repeat(np.exp2(scales.astype(np.float64) - 127.0), 8, axis=1)[..., None]
    return vals.transpose(0, 1, 3, 2).reshape(g * 512, n)

def pack4(w):
    words, scales = pack_weight(w, "e2m1")
    return words.reshape(words.shape[0], 128, -1), scales


def unpack4(words, scales):
    return unpack_weight(words.reshape(words.shape[0], 128, -1, 2), scales, "e2m1")


T, B, I, H = 32, 128, 512, 512


def sigmoid(v):
    return 1.0 / (1.0 + np.exp(-v))


def setup_inputs():
    s = mx_kscale(I)
    inp = bf(np.random.standard_normal((T, B, I)) * s)
    h0 = bf(np.random.standard_normal((B, H)))
    c0 = bf(np.random.standard_normal((B, H)))
    noise = bf(np.random.standard_normal((B, H)) * 0.3)
    w_ih = np.random.standard_normal((4 * H, I)) / np.sqrt(I) / s[None, :]
    words, scales = pack4(np.ascontiguousarray(w_ih.T))
    return {
        "input": inp,
        "h0": h0,
        "c0": c0,
        "noise": noise,
        "W_ih_words": words,
        "W_ih_scales": scales,
        "W_hh": bf(np.random.standard_normal((4 * H, H)) * 0.7 / np.sqrt(H)),
        "b_ih": bf(np.random.standard_normal(4 * H) * 0.3),
        "b_hh": bf(np.random.standard_normal(4 * H) * 0.3),
    }


def reference(input, h0, c0, noise, W_ih_words, W_ih_scales, W_hh, b_ih, b_hh):
    hsz = h0.shape[-1]
    gx = mxq(f64(input), 2, "e4m3") @ unpack4(W_ih_words, W_ih_scales)
    gh = f64(h0) @ f64(W_hh).T
    gates = gx + gh[None, :, :] + (f64(b_ih) + f64(b_hh))
    i_g = sigmoid(gates[..., 0 * hsz:1 * hsz])
    f_g = sigmoid(gates[..., 1 * hsz:2 * hsz])
    g_g = np.tanh(gates[..., 2 * hsz:3 * hsz])
    o_g = sigmoid(gates[..., 3 * hsz:4 * hsz])
    c = f_g * f64(c0)[None] + i_g * g_g
    h = o_g * np.tanh(c) + f64(noise)[None]
    return (h, np.stack([h[-1], c[-1]]))

@@ -1,0 +1,263 @@
+from contextlib import ExitStack
+
+import concourse.mybir as mybir
+from concourse.masks import make_identity
+
+F32 = mybir.dt.float32
+BF16 = mybir.dt.bfloat16
+I32 = mybir.dt.int32
+U8 = mybir.dt.uint8
+U32 = mybir.dt.uint32
+FP8X4 = mybir.dt.float8_e4m3fn_x4
+FP4X4 = mybir.dt.float4_e2m1fn_x4
+ACT = mybir.ActivationFunctionType
+ALU = mybir.AluOpType
+
+P = 128
+STEPS = 32
+K = 512
+H = 512
+GATES = 4
+GATE_I, GATE_F, GATE_G, GATE_O = 0, 1, 2, 3
+WORDS = K // 2
+STEPS_PER_LOAD = 4
+STEPS_PER_BANK = 2
+STEPS_PER_GROUP = 2
+GROUPS = STEPS // STEPS_PER_GROUP
+LOADS = STEPS // STEPS_PER_LOAD
+GROUPS_PER_LOAD = STEPS_PER_LOAD // STEPS_PER_GROUP
+GATE_ORDER = (GATE_F, GATE_I, GATE_G, GATE_O)
+
+FLOPS = 2 * STEPS * P * K * GATES * H + 2 * P * H * GATES * H
+
+
+def tile_lstmlayer_kernel(
+    tc, x, h0, c0, noise, w_ih_words, w_ih_scales, w_hh, b_ih, b_hh, out_h, out_state
+):
+    nc = tc.nc
+    with ExitStack() as ctx:
+        keep = ctx.enter_context(tc.tile_pool(name="keep", bufs=1))
+        stage = ctx.enter_context(tc.tile_pool(name="stage", bufs=2))
+        fixed_psum = ctx.enter_context(tc.psum_pool(name="fixed_psum", bufs=1))
+        psum = ctx.enter_context(tc.psum_pool(name="psum", bufs=6))
+
+        ident_f32 = keep.tile([P, P], F32)
+        make_identity(nc, ident_f32[:])
+        ident_bf16 = keep.tile([P, P], BF16)
+        make_identity(nc, ident_bf16[:])
+        ones = keep.tile([P, P], BF16)
+        nc.gpsimd.memset(ones[:], 1.0)
+
+        warm = keep.tile([P, 1], F32)
+        nc.vector.memset(warm[:], 0.0)
+        nc.scalar.activation(out=warm[:], in_=warm[:], func=ACT.Sigmoid)
+
+        bias_rows = keep.tile([P, GATES * H], BF16)
+        nc.vector.memset(bias_rows[:].bitcast(I32), 0)
+        w_scale_plane = keep.tile([P, GATES * H], U8, align_bytes=64)
+        nc.vector.memset(w_scale_plane[:].bitcast(I32), 0)
+
+        x_codes = keep.tile([P, STEPS, P], U32, align_bytes=64)
+        x_scales = keep.tile([P, STEPS, P], U8, align_bytes=64)
+        x_loads = []
+        grouped_tiles = {}
+
+        def load_x(c):
+            x_sb = keep.tile([P, STEPS_PER_LOAD, K], BF16, name="x_sb%d" % c)
+            nc.sync.dma_start(
+                out=x_sb[:],
+                in_=x[STEPS_PER_LOAD * c : STEPS_PER_LOAD * (c + 1)].rearrange("t b k -> b t k"),
+            )
+            x_loads.append(x_sb)
+
+        def regroup_x(c):
+            x_words = x_loads[c][:].rearrange("b s k -> b (s k)").bitcast(F32)
+            grouped = stage.tile([P, STEPS_PER_LOAD * P * 4], BF16, align_bytes=64, name="grouped")
+            grouped_tiles[c] = grouped
+            grouped_words = grouped[:].bitcast(F32).rearrange(
+                "p (s b u) -> p s b u", s=STEPS_PER_LOAD, u=2
+            )
+            for q in range(STEPS_PER_LOAD // STEPS_PER_BANK):
+                x_t_ps = psum.tile([P, STEPS_PER_BANK, 2, P], F32, tag="bank", name="x_t_ps")
+                for s in range(STEPS_PER_BANK):
+                    first = WORDS * (STEPS_PER_BANK * q + s)
+                    for u in range(2):
+                        nc.tensor.transpose(
+                            x_t_ps[:, s, u, :], x_words[:, first + u : first + WORDS : 2], ident_f32[:]
+                        )
+                nc.scalar.copy(
+                    out=grouped_words[:, STEPS_PER_BANK * q : STEPS_PER_BANK * (q + 1)],
+                    in_=x_t_ps[:].rearrange("p s u b -> p s b u"),
+                )
+
+        def quantise_x(c):
+            steps = slice(STEPS_PER_LOAD * c, STEPS_PER_LOAD * (c + 1))
+            nc.vector.quantize_mx(
+                out=x_codes[:, steps, :].rearrange("p s b -> p (s b)").bitcast(FP8X4),
+                scales=x_scales[:, steps, :].rearrange("p s b -> p (s b)"),
+                in_=grouped_tiles[c][:],
+            )
+
+        const = keep.tile([P, GATES, H], F32)
+        w_words = keep.tile([P, 2 * GATES * H], U8, align_bytes=64)
+        c0_sb = keep.tile([P, H], BF16)
+        noise_sb = keep.tile([P, H], BF16)
+        with tc.tile_pool(name="setup", bufs=1) as setup:
+            h0_sb = setup.tile([P, H], BF16)
+            whh_sb = setup.tile([P, GATES, 4, H], BF16)
+
+            def load_whh(j):
+                nc.sync.dma_start(
+                    out=whh_sb[:, j],
+                    in_=w_hh[H * j : H * (j + 1), :].rearrange("(p a) k -> p a k", a=4),
+                )
+
+            nc.sync.dma_start(out=h0_sb[:], in_=h0)
+            nc.sync.dma_start(out=bias_rows[0:1, :], in_=b_ih.rearrange("(o n) -> o n", o=1))
+            nc.sync.dma_start(out=bias_rows[1:2, :], in_=b_hh.rearrange("(o n) -> o n", o=1))
+            load_whh(GATE_ORDER[0])
+            load_x(0)
+            for quad in range(4):
+                nc.sync.dma_start(
+                    out=w_scale_plane[32 * quad : 32 * quad + 4, :].bitcast(I32),
+                    in_=w_ih_scales[0, 4 * quad : 4 * quad + 4, :].bitcast(I32),
+                )
+            nc.sync.dma_start(out=w_words[:].bitcast(I32), in_=w_ih_words[0].bitcast(I32))
+            for j in GATE_ORDER[1:]:
+                load_whh(j)
+            nc.sync.dma_start(out=c0_sb[:], in_=c0)
+            nc.sync.dma_start(out=noise_sb[:], in_=noise)
+            for c in range(1, LOADS):
+                load_x(c)
+
+            h0_t_ps = psum.tile([P, 2, P], F32, tag="bank")
+            for half in range(2):
+                nc.tensor.transpose(
+                    h0_t_ps[:, half, :], h0_sb[:].bitcast(F32)[:, P * half : P * (half + 1)], ident_f32[:]
+                )
+            h0_t = setup.tile([P, 2, P], F32)
+            nc.vector.tensor_copy(out=h0_t[:], in_=h0_t_ps[:])
+            whh_t = setup.tile([P, 2, GATES * H], F32)
+
+            def transpose_whh(j):
+                for half in range(2):
+                    whh_t_ps = psum.tile([P, 4, P], F32, tag="bank", name="whh_t_ps")
+                    for a in range(4):
+                        nc.tensor.transpose(
+                            whh_t_ps[:, a, :],
+                            whh_sb[:, j, a, :].bitcast(F32)[:, P * half : P * (half + 1)],
+                            ident_f32[:],
+                        )
+                    dst = whh_t[:, half, H * j : H * (j + 1)].rearrange("w (p a) -> w p a", a=4)
+                    src = whh_t_ps[:].rearrange("w a p -> w p a")
+                    if half == 0:
+                        nc.vector.tensor_copy(out=dst, in_=src)
+                    else:
+                        nc.scalar.copy(out=dst, in_=src)
+
+            def make_const(j):
+                const_ps = psum.tile([P, H], F32, tag="bank", name="const_ps")
+                for half in range(2):
+                    for e in range(2):
+                        nc.tensor.matmul(
+                            out=const_ps[:],
+                            lhsT=h0_t[:, half, :].bitcast(BF16).rearrange("w (b e) -> w b e", e=2)[:, :, e],
+                            rhs=whh_t[:, half, H * j : H * (j + 1)]
+                            .bitcast(BF16)
+                            .rearrange("w (n e) -> w n e", e=2)[:, :, e],
+                            start=(half == 0 and e == 0),
+                            stop=False,
+                        )
+                nc.tensor.matmul(
+                    out=const_ps[:], lhsT=ones[:], rhs=bias_rows[:, H * j : H * (j + 1)],
+                    start=False, stop=True,
+                )
+                nc.vector.tensor_copy(out=const[:, j, :], in_=const_ps[:])
+
+            transpose_whh(GATE_ORDER[0])
+            regroup_x(0)
+            for n in range(1, GATES):
+                transpose_whh(GATE_ORDER[n])
+                make_const(GATE_ORDER[n - 1])
+                if n == 1:
+                    quantise_x(0)
+            make_const(GATE_ORDER[GATES - 1])
+
+        c0_ps = fixed_psum.tile([P, H], F32)
+        nc.tensor.matmul(out=c0_ps[:], lhsT=ident_bf16[:], rhs=c0_sb[:], start=True, stop=True)
+        noise_ps = fixed_psum.tile([P, H], F32)
+        nc.tensor.matmul(out=noise_ps[:], lhsT=ident_bf16[:], rhs=noise_sb[:], start=True, stop=True)
+
+        work = ctx.enter_context(tc.tile_pool(name="work", bufs=2))
+        group_shape = [P, STEPS_PER_GROUP, H]
+        c0_bc = c0_ps[:].unsqueeze(1).to_broadcast(group_shape)
+        noise_bc = noise_ps[:].unsqueeze(1).to_broadcast(group_shape)
+        gates, cell, o_tanh_c = {}, {}, {}
+
+        def project(n):
+            gates[n] = work.tile([P, GATES, STEPS_PER_GROUP, H], F32, bufs=4, name="gates")
+            for gate in GATE_ORDER:
+                for s in range(STEPS_PER_GROUP):
+                    t = STEPS_PER_GROUP * n + s
+                    gate_ps = psum.tile([P, H], F32, tag="bank", name="gate_ps")
+                    nc.tensor.matmul_mx(
+                        out=gate_ps[:],
+                        lhsT=x_codes[:, t, :].bitcast(FP8X4),
+                        lhsT_scale=x_scales[:, t, :],
+                        rhs=w_words[:, 2 * H * gate : 2 * H * (gate + 1)].bitcast(FP4X4),
+                        rhs_scale=w_scale_plane[:, H * gate : H * (gate + 1)],
+                        start=True,
+                        stop=True,
+                    )
+                    nc.vector.tensor_tensor(
+                        out=gates[n][:, gate, s, :], in0=gate_ps[:], in1=const[:, gate, :], op=ALU.add
+                    )
+                nc.scalar.activation(
+                    out=gates[n][:, gate],
+                    in_=gates[n][:, gate],
+                    func=(ACT.Tanh if gate == GATE_G else ACT.Sigmoid),
+                )
+
+        def new_cell(n):
+            f_c0 = work.tile(group_shape, F32, name="f_c0")
+            nc.vector.tensor_tensor(out=f_c0[:], in0=gates[n][:, GATE_F], in1=c0_bc, op=ALU.mult)
+            i_g = work.tile(group_shape, F32, name="i_g")
+            nc.gpsimd.tensor_tensor(
+                out=i_g[:], in0=gates[n][:, GATE_I], in1=gates[n][:, GATE_G], op=ALU.mult
+            )
+            cell[n] = work.tile(group_shape, F32, name="cell")
+            nc.gpsimd.tensor_tensor(out=cell[n][:], in0=f_c0[:], in1=i_g[:], op=ALU.add)
+
+        def gate_cell(n):
+            tanh_c = work.tile(group_shape, F32, name="tanh_c")
+            nc.scalar.activation(out=tanh_c[:], in_=cell[n][:], func=ACT.Tanh)
+            o_tanh_c[n] = work.tile(group_shape, F32, name="o_tanh_c")
+            nc.gpsimd.tensor_tensor(
+                out=o_tanh_c[n][:], in0=gates[n][:, GATE_O], in1=tanh_c[:], op=ALU.mult
+            )
+
+        def store_h(n):
+            h = work.tile(group_shape, F32, name="h")
+            nc.vector.tensor_tensor(out=h[:], in0=o_tanh_c[n][:], in1=noise_bc, op=ALU.add)
+            nc.sync.dma_start(
+                out=out_h[STEPS_PER_GROUP * n : STEPS_PER_GROUP * (n + 1)].rearrange("t b m -> b t m"),
+                in_=h[:],
+            )
+            if n == GROUPS - 1:
+                nc.sync.dma_start(out=out_state[0], in_=h[:, STEPS_PER_GROUP - 1, :])
+                nc.sync.dma_start(out=out_state[1], in_=cell[n][:, STEPS_PER_GROUP - 1, :])
+
+        with tc.manual_schedule():
+            for n in range(GROUPS + 2):
+                next_load = n // GROUPS_PER_LOAD + 1
+                if n < GROUPS:
+                    project(n)
+                    if n % GROUPS_PER_LOAD == 1 and next_load < LOADS:
+                        quantise_x(next_load)
+                    new_cell(n)
+                if 1 <= n <= GROUPS:
+                    gate_cell(n - 1)
+                if n >= 2:
+                    store_h(n - 2)
+                if n % GROUPS_PER_LOAD == 0 and next_load < LOADS:
+                    regroup_x(next_load)

@@ -26,7 +26,8 @@ STEPS_PER_GROUP = 2
 GROUPS = STEPS // STEPS_PER_GROUP
 LOADS = STEPS // STEPS_PER_LOAD
 GROUPS_PER_LOAD = STEPS_PER_LOAD // STEPS_PER_GROUP
-GATE_ORDER = (GATE_F, GATE_I, GATE_G, GATE_O)
+GATE_ORDER = (GATE_I, GATE_G, GATE_F, GATE_O)
+GROUPS_WITHOUT_HELPER = 1
 
 FLOPS = 2 * STEPS * P * K * GATES * H + 2 * P * H * GATES * H
 
@@ -36,8 +37,10 @@ def tile_lstmlayer_kernel(
 ):
     nc = tc.nc
     with ExitStack() as ctx:
+        ctx.enter_context(tc.manual_schedule())
         keep = ctx.enter_context(tc.tile_pool(name="keep", bufs=1))
         stage = ctx.enter_context(tc.tile_pool(name="stage", bufs=2))
+        work = ctx.enter_context(tc.tile_pool(name="work", bufs=2))
         fixed_psum = ctx.enter_context(tc.psum_pool(name="fixed_psum", bufs=1))
         psum = ctx.enter_context(tc.psum_pool(name="psum", bufs=6))
 
@@ -102,139 +105,124 @@ def tile_lstmlayer_kernel(
         w_words = keep.tile([P, 2 * GATES * H], U8, align_bytes=64)
         c0_sb = keep.tile([P, H], BF16)
         noise_sb = keep.tile([P, H], BF16)
-        with tc.tile_pool(name="setup", bufs=1) as setup:
-            h0_sb = setup.tile([P, H], BF16)
-            whh_sb = setup.tile([P, GATES, 4, H], BF16)
+        h0_sb = keep.tile([P, H], BF16)
+        whh_sb = keep.tile([P, GATES, 4, H], BF16)
 
-            def load_whh(j):
-                nc.sync.dma_start(
-                    out=whh_sb[:, j],
-                    in_=w_hh[H * j : H * (j + 1), :].rearrange("(p a) k -> p a k", a=4),
-                )
+        def load_whh(j):
+            nc.sync.dma_start(
+                out=whh_sb[:, j],
+                in_=w_hh[H * j : H * (j + 1), :].rearrange("(p a) k -> p a k", a=4),
+            )
 
-            nc.sync.dma_start(out=h0_sb[:], in_=h0)
-            nc.sync.dma_start(out=bias_rows[0:1, :], in_=b_ih.rearrange("(o n) -> o n", o=1))
-            nc.sync.dma_start(out=bias_rows[1:2, :], in_=b_hh.rearrange("(o n) -> o n", o=1))
-            load_whh(GATE_ORDER[0])
-            load_x(0)
-            for quad in range(4):
-                nc.sync.dma_start(
-                    out=w_scale_plane[32 * quad : 32 * quad + 4, :].bitcast(I32),
-                    in_=w_ih_scales[0, 4 * quad : 4 * quad + 4, :].bitcast(I32),
-                )
-            nc.sync.dma_start(out=w_words[:].bitcast(I32), in_=w_ih_words[0].bitcast(I32))
-            for j in GATE_ORDER[1:]:
-                load_whh(j)
-            nc.sync.dma_start(out=c0_sb[:], in_=c0)
-            nc.sync.dma_start(out=noise_sb[:], in_=noise)
-            for c in range(1, LOADS):
-                load_x(c)
+        nc.sync.dma_start(out=h0_sb[:], in_=h0)
+        nc.sync.dma_start(out=bias_rows[0:1, :], in_=b_ih.rearrange("(o n) -> o n", o=1))
+        nc.sync.dma_start(out=bias_rows[1:2, :], in_=b_hh.rearrange("(o n) -> o n", o=1))
+        load_whh(GATE_ORDER[0])
+        load_x(0)
+        load_whh(GATE_ORDER[1])
+        for quad in range(4):
+            nc.sync.dma_start(
+                out=w_scale_plane[32 * quad : 32 * quad + 4, :].bitcast(I32),
+                in_=w_ih_scales[0, 4 * quad : 4 * quad + 4, :].bitcast(I32),
+            )
+        nc.sync.dma_start(out=w_words[:].bitcast(I32), in_=w_ih_words[0].bitcast(I32))
+        for j in GATE_ORDER[2:]:
+            load_whh(j)
+        nc.sync.dma_start(out=c0_sb[:], in_=c0)
+        nc.sync.dma_start(out=noise_sb[:], in_=noise)
+        for c in range(1, LOADS):
+            load_x(c)
 
-            h0_t_ps = psum.tile([P, 2, P], F32, tag="bank")
+        h0_t_ps = psum.tile([P, 2, P], F32, tag="bank")
+        for half in range(2):
+            nc.tensor.transpose(
+                h0_t_ps[:, half, :], h0_sb[:].bitcast(F32)[:, P * half : P * (half + 1)], ident_f32[:]
+            )
+        h0_t = keep.tile([P, 2, P], F32)
+        nc.vector.tensor_copy(out=h0_t[:], in_=h0_t_ps[:])
+        whh_t = keep.tile([P, 2, GATES * H], F32)
+
+        def transpose_whh(j):
             for half in range(2):
-                nc.tensor.transpose(
-                    h0_t_ps[:, half, :], h0_sb[:].bitcast(F32)[:, P * half : P * (half + 1)], ident_f32[:]
-                )
-            h0_t = setup.tile([P, 2, P], F32)
-            nc.vector.tensor_copy(out=h0_t[:], in_=h0_t_ps[:])
-            whh_t = setup.tile([P, 2, GATES * H], F32)
+                whh_t_ps = psum.tile([P, 4, P], F32, tag="bank", name="whh_t_ps")
+                for a in range(4):
+                    nc.tensor.transpose(
+                        whh_t_ps[:, a, :],
+                        whh_sb[:, j, a, :].bitcast(F32)[:, P * half : P * (half + 1)],
+                        ident_f32[:],
+                    )
+                dst = whh_t[:, half, H * j : H * (j + 1)].rearrange("w (p a) -> w p a", a=4)
+                src = whh_t_ps[:].rearrange("w a p -> w p a")
+                if half == 0:
+                    nc.vector.tensor_copy(out=dst, in_=src)
+                else:
+                    nc.scalar.copy(out=dst, in_=src)
 
-            def transpose_whh(j):
-                for half in range(2):
-                    whh_t_ps = psum.tile([P, 4, P], F32, tag="bank", name="whh_t_ps")
-                    for a in range(4):
-                        nc.tensor.transpose(
-                            whh_t_ps[:, a, :],
-                            whh_sb[:, j, a, :].bitcast(F32)[:, P * half : P * (half + 1)],
-                            ident_f32[:],
-                        )
-                    dst = whh_t[:, half, H * j : H * (j + 1)].rearrange("w (p a) -> w p a", a=4)
-                    src = whh_t_ps[:].rearrange("w a p -> w p a")
-                    if half == 0:
-                        nc.vector.tensor_copy(out=dst, in_=src)
-                    else:
-                        nc.scalar.copy(out=dst, in_=src)
+        def make_const(j):
+            const_ps = psum.tile([P, H], F32, tag="bank", name="const_ps")
+            nc.tensor.matmul(
+                out=const_ps[:], lhsT=ones[:], rhs=bias_rows[:, H * j : H * (j + 1)],
+                start=True, stop=False,
+            )
+            for half in range(2):
+                for e in range(2):
+                    nc.tensor.matmul(
+                        out=const_ps[:],
+                        lhsT=h0_t[:, half, :].bitcast(BF16).rearrange("w (b e) -> w b e", e=2)[:, :, e],
+                        rhs=whh_t[:, half, H * j : H * (j + 1)]
+                        .bitcast(BF16)
+                        .rearrange("w (n e) -> w n e", e=2)[:, :, e],
+                        start=False,
+                        stop=(half == 1 and e == 1),
+                    )
+            nc.vector.tensor_copy(out=const[:, j, :], in_=const_ps[:])
 
-            def make_const(j):
-                const_ps = psum.tile([P, H], F32, tag="bank", name="const_ps")
-                for half in range(2):
-                    for e in range(2):
-                        nc.tensor.matmul(
-                            out=const_ps[:],
-                            lhsT=h0_t[:, half, :].bitcast(BF16).rearrange("w (b e) -> w b e", e=2)[:, :, e],
-                            rhs=whh_t[:, half, H * j : H * (j + 1)]
-                            .bitcast(BF16)
-                            .rearrange("w (n e) -> w n e", e=2)[:, :, e],
-                            start=(half == 0 and e == 0),
-                            stop=False,
-                        )
-                nc.tensor.matmul(
-                    out=const_ps[:], lhsT=ones[:], rhs=bias_rows[:, H * j : H * (j + 1)],
-                    start=False, stop=True,
-                )
-                nc.vector.tensor_copy(out=const[:, j, :], in_=const_ps[:])
-
-            transpose_whh(GATE_ORDER[0])
-            regroup_x(0)
-            for n in range(1, GATES):
-                transpose_whh(GATE_ORDER[n])
-                make_const(GATE_ORDER[n - 1])
-                if n == 1:
-                    quantise_x(0)
-            make_const(GATE_ORDER[GATES - 1])
+        transpose_whh(GATE_ORDER[0])
+        regroup_x(0)
+        transpose_whh(GATE_ORDER[1])
+        quantise_x(0)
 
         c0_ps = fixed_psum.tile([P, H], F32)
-        nc.tensor.matmul(out=c0_ps[:], lhsT=ident_bf16[:], rhs=c0_sb[:], start=True, stop=True)
         noise_ps = fixed_psum.tile([P, H], F32)
-        nc.tensor.matmul(out=noise_ps[:], lhsT=ident_bf16[:], rhs=noise_sb[:], start=True, stop=True)
 
-        work = ctx.enter_context(tc.tile_pool(name="work", bufs=2))
+        def fix_in_psum():
+            nc.tensor.matmul(out=c0_ps[:], lhsT=ident_bf16[:], rhs=c0_sb[:], start=True, stop=True)
+            nc.tensor.matmul(out=noise_ps[:], lhsT=ident_bf16[:], rhs=noise_sb[:], start=True, stop=True)
+
         group_shape = [P, STEPS_PER_GROUP, H]
         c0_bc = c0_ps[:].unsqueeze(1).to_broadcast(group_shape)
         noise_bc = noise_ps[:].unsqueeze(1).to_broadcast(group_shape)
         gates, cell, o_tanh_c = {}, {}, {}
 
-        def project(n):
-            gates[n] = work.tile([P, GATES, STEPS_PER_GROUP, H], F32, bufs=4, name="gates")
-            for gate in GATE_ORDER:
-                for s in range(STEPS_PER_GROUP):
-                    t = STEPS_PER_GROUP * n + s
-                    gate_ps = psum.tile([P, H], F32, tag="bank", name="gate_ps")
-                    nc.tensor.matmul_mx(
-                        out=gate_ps[:],
-                        lhsT=x_codes[:, t, :].bitcast(FP8X4),
-                        lhsT_scale=x_scales[:, t, :],
-                        rhs=w_words[:, 2 * H * gate : 2 * H * (gate + 1)].bitcast(FP4X4),
-                        rhs_scale=w_scale_plane[:, H * gate : H * (gate + 1)],
-                        start=True,
-                        stop=True,
-                    )
-                    nc.vector.tensor_tensor(
-                        out=gates[n][:, gate, s, :], in0=gate_ps[:], in1=const[:, gate, :], op=ALU.add
-                    )
-                nc.scalar.activation(
-                    out=gates[n][:, gate],
-                    in_=gates[n][:, gate],
-                    func=(ACT.Tanh if gate == GATE_G else ACT.Sigmoid),
+        def project(n, gate):
+            if n == 0:
+                make_const(gate)
+            for s in range(STEPS_PER_GROUP):
+                t = STEPS_PER_GROUP * n + s
+                gate_ps = psum.tile([P, H], F32, tag="bank", name="gate_ps")
+                nc.tensor.matmul_mx(
+                    out=gate_ps[:],
+                    lhsT=x_codes[:, t, :].bitcast(FP8X4),
+                    lhsT_scale=x_scales[:, t, :],
+                    rhs=w_words[:, 2 * H * gate : 2 * H * (gate + 1)].bitcast(FP4X4),
+                    rhs_scale=w_scale_plane[:, H * gate : H * (gate + 1)],
+                    start=True,
+                    stop=True,
                 )
-
-        def new_cell(n):
-            f_c0 = work.tile(group_shape, F32, name="f_c0")
-            nc.vector.tensor_tensor(out=f_c0[:], in0=gates[n][:, GATE_F], in1=c0_bc, op=ALU.mult)
-            i_g = work.tile(group_shape, F32, name="i_g")
-            nc.gpsimd.tensor_tensor(
-                out=i_g[:], in0=gates[n][:, GATE_I], in1=gates[n][:, GATE_G], op=ALU.mult
+                nc.vector.tensor_tensor(
+                    out=gates[n][:, gate, s, :], in0=gate_ps[:], in1=const[:, gate, :], op=ALU.add
+                )
+            nc.scalar.activation(
+                out=gates[n][:, gate],
+                in_=gates[n][:, gate],
+                func=(ACT.Tanh if gate == GATE_G else ACT.Sigmoid),
             )
-            cell[n] = work.tile(group_shape, F32, name="cell")
-            nc.gpsimd.tensor_tensor(out=cell[n][:], in0=f_c0[:], in1=i_g[:], op=ALU.add)
+            place = GATE_ORDER.index(gate)
+            if n == 0 and place + 2 < GATES:
+                transpose_whh(GATE_ORDER[place + 2])
 
-        def gate_cell(n):
-            tanh_c = work.tile(group_shape, F32, name="tanh_c")
-            nc.scalar.activation(out=tanh_c[:], in_=cell[n][:], func=ACT.Tanh)
-            o_tanh_c[n] = work.tile(group_shape, F32, name="o_tanh_c")
-            nc.gpsimd.tensor_tensor(
-                out=o_tanh_c[n][:], in0=gates[n][:, GATE_O], in1=tanh_c[:], op=ALU.mult
-            )
+        def helper(n):
+            return nc.vector if n >= GROUPS - GROUPS_WITHOUT_HELPER else nc.gpsimd
 
         def store_h(n):
             h = work.tile(group_shape, F32, name="h")
@@ -247,17 +235,36 @@ def tile_lstmlayer_kernel(
                 nc.sync.dma_start(out=out_state[0], in_=h[:, STEPS_PER_GROUP - 1, :])
                 nc.sync.dma_start(out=out_state[1], in_=cell[n][:, STEPS_PER_GROUP - 1, :])
 
-        with tc.manual_schedule():
-            for n in range(GROUPS + 2):
-                next_load = n // GROUPS_PER_LOAD + 1
-                if n < GROUPS:
-                    project(n)
-                    if n % GROUPS_PER_LOAD == 1 and next_load < LOADS:
-                        quantise_x(next_load)
-                    new_cell(n)
-                if 1 <= n <= GROUPS:
-                    gate_cell(n - 1)
-                if n >= 2:
-                    store_h(n - 2)
-                if n % GROUPS_PER_LOAD == 0 and next_load < LOADS:
-                    regroup_x(next_load)
+        for n in range(GROUPS + 2):
+            next_load = n // GROUPS_PER_LOAD + 1
+            if n < GROUPS:
+                gates[n] = work.tile([P, GATES, STEPS_PER_GROUP, H], F32, bufs=4, name="gates")
+                project(n, GATE_I)
+                project(n, GATE_G)
+                i_g = work.tile(group_shape, F32, name="i_g")
+                nc.gpsimd.tensor_tensor(
+                    out=i_g[:], in0=gates[n][:, GATE_I], in1=gates[n][:, GATE_G], op=ALU.mult
+                )
+                project(n, GATE_F)
+            if n >= 2:
+                store_h(n - 2)
+            if 1 <= n <= GROUPS:
+                tanh_c = work.tile(group_shape, F32, name="tanh_c")
+                nc.scalar.activation(out=tanh_c[:], in_=cell[n - 1][:], func=ACT.Tanh)
+                o_tanh_c[n - 1] = work.tile(group_shape, F32, name="o_tanh_c")
+                helper(n - 1).tensor_tensor(
+                    out=o_tanh_c[n - 1][:], in0=gates[n - 1][:, GATE_O], in1=tanh_c[:], op=ALU.mult
+                )
+            if n < GROUPS:
+                project(n, GATE_O)
+                if n % GROUPS_PER_LOAD == 1 and next_load < LOADS:
+                    quantise_x(next_load)
+            if n == 0:
+                fix_in_psum()
+            if n < GROUPS:
+                f_c0 = work.tile(group_shape, F32, name="f_c0")
+                nc.vector.tensor_tensor(out=f_c0[:], in0=gates[n][:, GATE_F], in1=c0_bc, op=ALU.mult)
+                cell[n] = work.tile(group_shape, F32, name="cell")
+                helper(n).tensor_tensor(out=cell[n][:], in0=f_c0[:], in1=i_g[:], op=ALU.add)
+            if n % GROUPS_PER_LOAD == 0 and next_load < LOADS:
+                regroup_x(next_load)

@@ -115,10 +115,10 @@ def tile_lstmlayer_kernel(
             )
 
         nc.sync.dma_start(out=h0_sb[:], in_=h0)
-        nc.sync.dma_start(out=bias_rows[0:1, :], in_=b_ih.rearrange("(o n) -> o n", o=1))
-        nc.sync.dma_start(out=bias_rows[1:2, :], in_=b_hh.rearrange("(o n) -> o n", o=1))
         load_whh(GATE_ORDER[0])
         load_x(0)
+        nc.sync.dma_start(out=bias_rows[0:1, :], in_=b_ih.rearrange("(o n) -> o n", o=1))
+        nc.sync.dma_start(out=bias_rows[1:2, :], in_=b_hh.rearrange("(o n) -> o n", o=1))
         load_whh(GATE_ORDER[1])
         for quad in range(4):
             nc.sync.dma_start(
@@ -160,10 +160,6 @@ def tile_lstmlayer_kernel(
 
         def make_const(j):
             const_ps = psum.tile([P, H], F32, tag="bank", name="const_ps")
-            nc.tensor.matmul(
-                out=const_ps[:], lhsT=ones[:], rhs=bias_rows[:, H * j : H * (j + 1)],
-                start=True, stop=False,
-            )
             for half in range(2):
                 for e in range(2):
                     nc.tensor.matmul(
@@ -172,9 +168,12 @@ def tile_lstmlayer_kernel(
                         rhs=whh_t[:, half, H * j : H * (j + 1)]
                         .bitcast(BF16)
                         .rearrange("w (n e) -> w n e", e=2)[:, :, e],
-                        start=False,
-                        stop=(half == 1 and e == 1),
+                        start=(half == 0 and e == 0),
+                        stop=False,
                     )
+            nc.tensor.matmul(
+                out=const_ps[:], lhsT=ones[:], rhs=bias_rows[:, H * j : H * (j + 1)], start=False, stop=True
+            )
             nc.vector.tensor_copy(out=const[:, j, :], in_=const_ps[:])
 
         transpose_whh(GATE_ORDER[0])
@@ -224,16 +223,24 @@ def tile_lstmlayer_kernel(
         def helper(n):
             return nc.vector if n >= GROUPS - GROUPS_WITHOUT_HELPER else nc.gpsimd
 
+        def pieces(n):
+            if n < GROUPS - 1:
+                return [slice(0, STEPS_PER_GROUP)]
+            return [slice(s, s + 1) for s in range(STEPS_PER_GROUP)]
+
         def store_h(n):
             h = work.tile(group_shape, F32, name="h")
-            nc.vector.tensor_tensor(out=h[:], in0=o_tanh_c[n][:], in1=noise_bc, op=ALU.add)
-            nc.sync.dma_start(
-                out=out_h[STEPS_PER_GROUP * n : STEPS_PER_GROUP * (n + 1)].rearrange("t b m -> b t m"),
-                in_=h[:],
-            )
+            for steps in pieces(n):
+                nc.vector.tensor_tensor(
+                    out=h[:, steps], in0=o_tanh_c[n][:, steps], in1=noise_bc[:, steps], op=ALU.add
+                )
+                first = STEPS_PER_GROUP * n
+                nc.sync.dma_start(
+                    out=out_h[first + steps.start : first + steps.stop].rearrange("t b m -> b t m"),
+                    in_=h[:, steps],
+                )
             if n == GROUPS - 1:
-                nc.sync.dma_start(out=out_state[0], in_=h[:, STEPS_PER_GROUP - 1, :])
-                nc.sync.dma_start(out=out_state[1], in_=cell[n][:, STEPS_PER_GROUP - 1, :])
+                nc.scalar.dma_start(out=out_state[0], in_=h[:, STEPS_PER_GROUP - 1, :])
 
         for n in range(GROUPS + 2):
             next_load = n // GROUPS_PER_LOAD + 1
@@ -250,11 +257,16 @@ def tile_lstmlayer_kernel(
                 store_h(n - 2)
             if 1 <= n <= GROUPS:
                 tanh_c = work.tile(group_shape, F32, name="tanh_c")
-                nc.scalar.activation(out=tanh_c[:], in_=cell[n - 1][:], func=ACT.Tanh)
                 o_tanh_c[n - 1] = work.tile(group_shape, F32, name="o_tanh_c")
-                helper(n - 1).tensor_tensor(
-                    out=o_tanh_c[n - 1][:], in0=gates[n - 1][:, GATE_O], in1=tanh_c[:], op=ALU.mult
-                )
+                for steps in pieces(n - 1):
+                    nc.scalar.activation(out=tanh_c[:, steps], in_=cell[n - 1][:, steps], func=ACT.Tanh)
+                for steps in pieces(n - 1):
+                    helper(n - 1).tensor_tensor(
+                        out=o_tanh_c[n - 1][:, steps],
+                        in0=gates[n - 1][:, GATE_O, steps],
+                        in1=tanh_c[:, steps],
+                        op=ALU.mult,
+                    )
             if n < GROUPS:
                 project(n, GATE_O)
                 if n % GROUPS_PER_LOAD == 1 and next_load < LOADS:
@@ -265,6 +277,9 @@ def tile_lstmlayer_kernel(
                 f_c0 = work.tile(group_shape, F32, name="f_c0")
                 nc.vector.tensor_tensor(out=f_c0[:], in0=gates[n][:, GATE_F], in1=c0_bc, op=ALU.mult)
                 cell[n] = work.tile(group_shape, F32, name="cell")
-                helper(n).tensor_tensor(out=cell[n][:], in0=f_c0[:], in1=i_g[:], op=ALU.add)
+                for steps in pieces(n):
+                    helper(n).tensor_tensor(out=cell[n][:, steps], in0=f_c0[:, steps], in1=i_g[:, steps], op=ALU.add)
+                if n == GROUPS - 1:
+                    nc.scalar.dma_start(out=out_state[1], in_=cell[n][:, STEPS_PER_GROUP - 1, :])
             if n % GROUPS_PER_LOAD == 0 and next_load < LOADS:
                 regroup_x(next_load)

@@ -28,6 +28,7 @@ LOADS = STEPS // STEPS_PER_LOAD
 GROUPS_PER_LOAD = STEPS_PER_LOAD // STEPS_PER_GROUP
 GATE_ORDER = (GATE_I, GATE_G, GATE_F, GATE_O)
 GROUPS_WITHOUT_HELPER = 1
+WARM_UP = 6
 
 FLOPS = 2 * STEPS * P * K * GATES * H + 2 * P * H * GATES * H
 
@@ -59,6 +60,10 @@ def tile_lstmlayer_kernel(
         nc.vector.memset(bias_rows[:].bitcast(I32), 0)
         w_scale_plane = keep.tile([P, GATES * H], U8, align_bytes=64)
         nc.vector.memset(w_scale_plane[:].bitcast(I32), 0)
+
+        warm_ps = psum.tile([P, H], F32, tag="bank", name="warm_ps")
+        for k in range(WARM_UP):
+            nc.tensor.matmul(out=warm_ps[:, 0:P], lhsT=ident_f32[:], rhs=ident_f32[:], start=True, stop=True)
 
         x_codes = keep.tile([P, STEPS, P], U32, align_bytes=64)
         x_scales = keep.tile([P, STEPS, P], U8, align_bytes=64)
@@ -140,6 +145,10 @@ def tile_lstmlayer_kernel(
             )
         h0_t = keep.tile([P, 2, P], F32)
         nc.vector.tensor_copy(out=h0_t[:], in_=h0_t_ps[:])
+        h0_rows = keep.tile([P, 2, 2, P], BF16)
+        nc.vector.tensor_copy(
+            out=h0_rows[:], in_=h0_t[:].bitcast(BF16).rearrange("w half (b e) -> w half e b", e=2)
+        )
         whh_t = keep.tile([P, 2, GATES * H], F32)
 
         def transpose_whh(j):
@@ -164,7 +173,7 @@ def tile_lstmlayer_kernel(
                 for e in range(2):
                     nc.tensor.matmul(
                         out=const_ps[:],
-                        lhsT=h0_t[:, half, :].bitcast(BF16).rearrange("w (b e) -> w b e", e=2)[:, :, e],
+                        lhsT=h0_rows[:, half, e, :],
                         rhs=whh_t[:, half, H * j : H * (j + 1)]
                         .bitcast(BF16)
                         .rearrange("w (n e) -> w n e", e=2)[:, :, e],

@@ -122,15 +122,15 @@ def tile_lstmlayer_kernel(
         nc.sync.dma_start(out=h0_sb[:], in_=h0)
         load_whh(GATE_ORDER[0])
         load_x(0)
+        load_whh(GATE_ORDER[1])
+        nc.sync.dma_start(out=w_words[:].bitcast(I32), in_=w_ih_words[0].bitcast(I32))
         nc.sync.dma_start(out=bias_rows[0:1, :], in_=b_ih.rearrange("(o n) -> o n", o=1))
         nc.sync.dma_start(out=bias_rows[1:2, :], in_=b_hh.rearrange("(o n) -> o n", o=1))
-        load_whh(GATE_ORDER[1])
         for quad in range(4):
             nc.sync.dma_start(
                 out=w_scale_plane[32 * quad : 32 * quad + 4, :].bitcast(I32),
                 in_=w_ih_scales[0, 4 * quad : 4 * quad + 4, :].bitcast(I32),
             )
-        nc.sync.dma_start(out=w_words[:].bitcast(I32), in_=w_ih_words[0].bitcast(I32))
         for j in GATE_ORDER[2:]:
             load_whh(j)
         nc.sync.dma_start(out=c0_sb[:], in_=c0)

from contextlib import ExitStack

import concourse.mybir as mybir
from concourse.masks import make_identity

F32 = mybir.dt.float32
BF16 = mybir.dt.bfloat16
I32 = mybir.dt.int32
U8 = mybir.dt.uint8
U32 = mybir.dt.uint32
FP8X4 = mybir.dt.float8_e4m3fn_x4
FP4X4 = mybir.dt.float4_e2m1fn_x4
ACT = mybir.ActivationFunctionType
ALU = mybir.AluOpType

P = 128
STEPS = 32
K = 512
H = 512
GATES = 4
GATE_I, GATE_F, GATE_G, GATE_O = 0, 1, 2, 3
WORDS = K // 2
STEPS_PER_LOAD = 4
STEPS_PER_BANK = 2
STEPS_PER_GROUP = 2
GROUPS = STEPS // STEPS_PER_GROUP
LOADS = STEPS // STEPS_PER_LOAD
GROUPS_PER_LOAD = STEPS_PER_LOAD // STEPS_PER_GROUP
GATE_ORDER = (GATE_I, GATE_G, GATE_F, GATE_O)
GROUPS_WITHOUT_HELPER = 1
WARM_UP = 6

FLOPS = 2 * STEPS * P * K * GATES * H + 2 * P * H * GATES * H


def tile_lstmlayer_kernel(
    tc, x, h0, c0, noise, w_ih_words, w_ih_scales, w_hh, b_ih, b_hh, out_h, out_state
):
    nc = tc.nc
    with ExitStack() as ctx:
        ctx.enter_context(tc.manual_schedule())
        keep = ctx.enter_context(tc.tile_pool(name="keep", bufs=1))
        stage = ctx.enter_context(tc.tile_pool(name="stage", bufs=2))
        work = ctx.enter_context(tc.tile_pool(name="work", bufs=2))
        fixed_psum = ctx.enter_context(tc.psum_pool(name="fixed_psum", bufs=1))
        psum = ctx.enter_context(tc.psum_pool(name="psum", bufs=6))

        ident_f32 = keep.tile([P, P], F32)
        make_identity(nc, ident_f32[:])
        ident_bf16 = keep.tile([P, P], BF16)
        make_identity(nc, ident_bf16[:])
        ones = keep.tile([P, P], BF16)
        nc.gpsimd.memset(ones[:], 1.0)

        warm = keep.tile([P, 1], F32)
        nc.vector.memset(warm[:], 0.0)
        nc.scalar.activation(out=warm[:], in_=warm[:], func=ACT.Sigmoid)

        bias_rows = keep.tile([P, GATES * H], BF16)
        nc.vector.memset(bias_rows[:].bitcast(I32), 0)
        w_scale_plane = keep.tile([P, GATES * H], U8, align_bytes=64)
        nc.vector.memset(w_scale_plane[:].bitcast(I32), 0)

        warm_ps = psum.tile([P, H], F32, tag="bank", name="warm_ps")
        for k in range(WARM_UP):
            nc.tensor.matmul(out=warm_ps[:, 0:P], lhsT=ident_f32[:], rhs=ident_f32[:], start=True, stop=True)

        x_codes = keep.tile([P, STEPS, P], U32, align_bytes=64)
        x_scales = keep.tile([P, STEPS, P], U8, align_bytes=64)
        x_loads = []
        grouped_tiles = {}

        def load_x(c):
            x_sb = keep.tile([P, STEPS_PER_LOAD, K], BF16, name="x_sb%d" % c)
            nc.sync.dma_start(
                out=x_sb[:],
                in_=x[STEPS_PER_LOAD * c : STEPS_PER_LOAD * (c + 1)].rearrange("t b k -> b t k"),
            )
            x_loads.append(x_sb)

        def regroup_x(c):
            x_words = x_loads[c][:].rearrange("b s k -> b (s k)").bitcast(F32)
            grouped = stage.tile([P, STEPS_PER_LOAD * P * 4], BF16, align_bytes=64, name="grouped")
            grouped_tiles[c] = grouped
            grouped_words = grouped[:].bitcast(F32).rearrange(
                "p (s b u) -> p s b u", s=STEPS_PER_LOAD, u=2
            )
            for q in range(STEPS_PER_LOAD // STEPS_PER_BANK):
                x_t_ps = psum.tile([P, STEPS_PER_BANK, 2, P], F32, tag="bank", name="x_t_ps")
                for s in range(STEPS_PER_BANK):
                    first = WORDS * (STEPS_PER_BANK * q + s)
                    for u in range(2):
                        nc.tensor.transpose(
                            x_t_ps[:, s, u, :], x_words[:, first + u : first + WORDS : 2], ident_f32[:]
                        )
                nc.scalar.copy(
                    out=grouped_words[:, STEPS_PER_BANK * q : STEPS_PER_BANK * (q + 1)],
                    in_=x_t_ps[:].rearrange("p s u b -> p s b u"),
                )

        def quantise_x(c):
            steps = slice(STEPS_PER_LOAD * c, STEPS_PER_LOAD * (c + 1))
            nc.vector.quantize_mx(
                out=x_codes[:, steps, :].rearrange("p s b -> p (s b)").bitcast(FP8X4),
                scales=x_scales[:, steps, :].rearrange("p s b -> p (s b)"),
                in_=grouped_tiles[c][:],
            )

        const = keep.tile([P, GATES, H], F32)
        w_words = keep.tile([P, 2 * GATES * H], U8, align_bytes=64)
        c0_sb = keep.tile([P, H], BF16)
        noise_sb = keep.tile([P, H], BF16)
        h0_sb = keep.tile([P, H], BF16)
        whh_sb = keep.tile([P, GATES, 4, H], BF16)

        def load_whh(j):
            nc.sync.dma_start(
                out=whh_sb[:, j],
                in_=w_hh[H * j : H * (j + 1), :].rearrange("(p a) k -> p a k", a=4),
            )

        nc.sync.dma_start(out=h0_sb[:], in_=h0)
        load_whh(GATE_ORDER[0])
        load_x(0)
        load_whh(GATE_ORDER[1])
        nc.sync.dma_start(out=w_words[:].bitcast(I32), in_=w_ih_words[0].bitcast(I32))
        nc.sync.dma_start(out=bias_rows[0:1, :], in_=b_ih.rearrange("(o n) -> o n", o=1))
        nc.sync.dma_start(out=bias_rows[1:2, :], in_=b_hh.rearrange("(o n) -> o n", o=1))
        for quad in range(4):
            nc.sync.dma_start(
                out=w_scale_plane[32 * quad : 32 * quad + 4, :].bitcast(I32),
                in_=w_ih_scales[0, 4 * quad : 4 * quad + 4, :].bitcast(I32),
            )
        for j in GATE_ORDER[2:]:
            load_whh(j)
        nc.sync.dma_start(out=c0_sb[:], in_=c0)
        nc.sync.dma_start(out=noise_sb[:], in_=noise)
        for c in range(1, LOADS):
            load_x(c)

        h0_t_ps = psum.tile([P, 2, P], F32, tag="bank")
        for half in range(2):
            nc.tensor.transpose(
                h0_t_ps[:, half, :], h0_sb[:].bitcast(F32)[:, P * half : P * (half + 1)], ident_f32[:]
            )
        h0_t = keep.tile([P, 2, P], F32)
        nc.vector.tensor_copy(out=h0_t[:], in_=h0_t_ps[:])
        h0_rows = keep.tile([P, 2, 2, P], BF16)
        nc.vector.tensor_copy(
            out=h0_rows[:], in_=h0_t[:].bitcast(BF16).rearrange("w half (b e) -> w half e b", e=2)
        )
        whh_t = keep.tile([P, 2, GATES * H], F32)

        def transpose_whh(j):
            for half in range(2):
                whh_t_ps = psum.tile([P, 4, P], F32, tag="bank", name="whh_t_ps")
                for a in range(4):
                    nc.tensor.transpose(
                        whh_t_ps[:, a, :],
                        whh_sb[:, j, a, :].bitcast(F32)[:, P * half : P * (half + 1)],
                        ident_f32[:],
                    )
                dst = whh_t[:, half, H * j : H * (j + 1)].rearrange("w (p a) -> w p a", a=4)
                src = whh_t_ps[:].rearrange("w a p -> w p a")
                if half == 0:
                    nc.vector.tensor_copy(out=dst, in_=src)
                else:
                    nc.scalar.copy(out=dst, in_=src)

        def make_const(j):
            const_ps = psum.tile([P, H], F32, tag="bank", name="const_ps")
            for half in range(2):
                for e in range(2):
                    nc.tensor.matmul(
                        out=const_ps[:],
                        lhsT=h0_rows[:, half, e, :],
                        rhs=whh_t[:, half, H * j : H * (j + 1)]
                        .bitcast(BF16)
                        .rearrange("w (n e) -> w n e", e=2)[:, :, e],
                        start=(half == 0 and e == 0),
                        stop=False,
                    )
            nc.tensor.matmul(
                out=const_ps[:], lhsT=ones[:], rhs=bias_rows[:, H * j : H * (j + 1)], start=False, stop=True
            )
            nc.vector.tensor_copy(out=const[:, j, :], in_=const_ps[:])

        transpose_whh(GATE_ORDER[0])
        regroup_x(0)
        transpose_whh(GATE_ORDER[1])
        quantise_x(0)

        c0_ps = fixed_psum.tile([P, H], F32)
        noise_ps = fixed_psum.tile([P, H], F32)

        def fix_in_psum():
            nc.tensor.matmul(out=c0_ps[:], lhsT=ident_bf16[:], rhs=c0_sb[:], start=True, stop=True)
            nc.tensor.matmul(out=noise_ps[:], lhsT=ident_bf16[:], rhs=noise_sb[:], start=True, stop=True)

        group_shape = [P, STEPS_PER_GROUP, H]
        c0_bc = c0_ps[:].unsqueeze(1).to_broadcast(group_shape)
        noise_bc = noise_ps[:].unsqueeze(1).to_broadcast(group_shape)
        gates, cell, o_tanh_c = {}, {}, {}

        def project(n, gate):
            if n == 0:
                make_const(gate)
            for s in range(STEPS_PER_GROUP):
                t = STEPS_PER_GROUP * n + s
                gate_ps = psum.tile([P, H], F32, tag="bank", name="gate_ps")
                nc.tensor.matmul_mx(
                    out=gate_ps[:],
                    lhsT=x_codes[:, t, :].bitcast(FP8X4),
                    lhsT_scale=x_scales[:, t, :],
                    rhs=w_words[:, 2 * H * gate : 2 * H * (gate + 1)].bitcast(FP4X4),
                    rhs_scale=w_scale_plane[:, H * gate : H * (gate + 1)],
                    start=True,
                    stop=True,
                )
                nc.vector.tensor_tensor(
                    out=gates[n][:, gate, s, :], in0=gate_ps[:], in1=const[:, gate, :], op=ALU.add
                )
            nc.scalar.activation(
                out=gates[n][:, gate],
                in_=gates[n][:, gate],
                func=(ACT.Tanh if gate == GATE_G else ACT.Sigmoid),
            )
            place = GATE_ORDER.index(gate)
            if n == 0 and place + 2 < GATES:
                transpose_whh(GATE_ORDER[place + 2])

        def helper(n):
            return nc.vector if n >= GROUPS - GROUPS_WITHOUT_HELPER else nc.gpsimd

        def pieces(n):
            if n < GROUPS - 1:
                return [slice(0, STEPS_PER_GROUP)]
            return [slice(s, s + 1) for s in range(STEPS_PER_GROUP)]

        def store_h(n):
            h = work.tile(group_shape, F32, name="h")
            for steps in pieces(n):
                nc.vector.tensor_tensor(
                    out=h[:, steps], in0=o_tanh_c[n][:, steps], in1=noise_bc[:, steps], op=ALU.add
                )
                first = STEPS_PER_GROUP * n
                nc.sync.dma_start(
                    out=out_h[first + steps.start : first + steps.stop].rearrange("t b m -> b t m"),
                    in_=h[:, steps],
                )
            if n == GROUPS - 1:
                nc.scalar.dma_start(out=out_state[0], in_=h[:, STEPS_PER_GROUP - 1, :])

        for n in range(GROUPS + 2):
            next_load = n // GROUPS_PER_LOAD + 1
            if n < GROUPS:
                gates[n] = work.tile([P, GATES, STEPS_PER_GROUP, H], F32, bufs=4, name="gates")
                project(n, GATE_I)
                project(n, GATE_G)
                i_g = work.tile(group_shape, F32, name="i_g")
                nc.gpsimd.tensor_tensor(
                    out=i_g[:], in0=gates[n][:, GATE_I], in1=gates[n][:, GATE_G], op=ALU.mult
                )
                project(n, GATE_F)
            if n >= 2:
                store_h(n - 2)
            if 1 <= n <= GROUPS:
                tanh_c = work.tile(group_shape, F32, name="tanh_c")
                o_tanh_c[n - 1] = work.tile(group_shape, F32, name="o_tanh_c")
                for steps in pieces(n - 1):
                    nc.scalar.activation(out=tanh_c[:, steps], in_=cell[n - 1][:, steps], func=ACT.Tanh)
                for steps in pieces(n - 1):
                    helper(n - 1).tensor_tensor(
                        out=o_tanh_c[n - 1][:, steps],
                        in0=gates[n - 1][:, GATE_O, steps],
                        in1=tanh_c[:, steps],
                        op=ALU.mult,
                    )
            if n < GROUPS:
                project(n, GATE_O)
                if n % GROUPS_PER_LOAD == 1 and next_load < LOADS:
                    quantise_x(next_load)
            if n == 0:
                fix_in_psum()
            if n < GROUPS:
                f_c0 = work.tile(group_shape, F32, name="f_c0")
                nc.vector.tensor_tensor(out=f_c0[:], in0=gates[n][:, GATE_F], in1=c0_bc, op=ALU.mult)
                cell[n] = work.tile(group_shape, F32, name="cell")
                for steps in pieces(n):
                    helper(n).tensor_tensor(out=cell[n][:, steps], in0=f_c0[:, steps], in1=i_g[:, steps], op=ALU.add)
                if n == GROUPS - 1:
                    nc.scalar.dma_start(out=out_state[1], in_=cell[n][:, STEPS_PER_GROUP - 1, :])
            if n % GROUPS_PER_LOAD == 0 and next_load < LOADS:
                regroup_x(next_load)
